import numpy as np
import ml_dtypes

BF16 = ml_dtypes.bfloat16


def bf(x):
    return np.asarray(x, np.float32).astype(BF16)


def f32(x):
    return np.asarray(x, np.float32)


def f64(x):
    return np.asarray(x).astype(np.float64)


def striped(idx):
    return np.tile(idx.reshape(-1, 16).T, (8, 1))


C, V, N = 768, 1024, 512


def positional():
    pos = np.arange(N, dtype=np.float64)[None, :]
    denom = (10000.0 ** (2.0 * np.arange(C, dtype=np.float64) / C))[:, None]
    pe = pos / denom
    pe[0::2, 1:] = np.sin(pe[0::2, 1:])
    pe[1::2, 1:] = np.cos(pe[1::2, 1:])
    return pe


def setup_inputs():
    return {"table": f32(np.random.standard_normal((C, V))), "pe": f32(positional()), "se_b": f32(0.5 * np.random.standard_normal((C, 1))), "we": bf(np.random.standard_normal((C, V)) / np.sqrt(C)), "be": f32(0.5 * np.random.standard_normal((1, V))), "offs": striped(np.random.permutation(np.tile(np.arange(V), 2))[:N])}


def reference(table, pe, se_b, we, be, offs):
    idx = offs[:16].T.reshape(-1)
    x = f64(table)[:, idx] + f64(pe) + f64(se_b)
    z = x.T @ f64(we) + f64(be)
    return z - np.log(np.sum(np.exp(z), axis=1, keepdims=True))

@@ -1,0 +1,88 @@
+import concourse.mybir as mybir
+
+F32 = mybir.dt.float32
+BF16 = mybir.dt.bfloat16
+U16 = mybir.dt.uint16
+ALU = mybir.AluOpType
+ACT = mybir.ActivationFunctionType
+AXIS = mybir.AxisListType
+
+P = 128
+C, V, N = 768, 1024, 512
+CB = C // P
+TB = N // P
+BANK = 512
+VH = V // BANK
+
+FLOPS = 2 * N * C * V
+
+
+def tile_albertwithsoftmax_kernel(tc, table, pe, se_b, we, be, offs, out):
+    nc = tc.nc
+    with (
+        tc.tile_pool(name="held", bufs=1) as held,
+        tc.tile_pool(name="rows", bufs=2) as rows,
+        tc.tile_pool(name="stats", bufs=4) as stats,
+        tc.psum_pool(name="psum", bufs=1) as psum,
+    ):
+        offsets = held.tile([P, N // 16], U16, name="offsets")
+        nc.sync.dma_start(offsets[:], offs)
+        seb_row = held.tile([1, C], F32, name="seb_row")
+        nc.scalar.dma_start(seb_row[:], se_b.rearrange("c o -> o c"))
+
+        table_sb = [held.tile([P, V], F32, name=f"table{k}") for k in range(CB)]
+        pe_sb = [held.tile([P, N], F32, name=f"pe{k}") for k in range(CB)]
+        we_sb = [held.tile([P, V], BF16, name=f"we{k}") for k in range(CB)]
+        for k in range(CB):
+            block = slice(k * P, (k + 1) * P)
+            nc.sync.dma_start(table_sb[k][:], table[block, :])
+            nc.scalar.dma_start(pe_sb[k][:], pe[block, :])
+            nc.scalar.dma_start(we_sb[k][:], we[block, :])
+        be_all = held.tile([P, V], F32, name="be_all")
+        nc.scalar.dma_start(be_all[:], be.rearrange("o v -> (o v)").partition_broadcast(P))
+
+        one = held.tile([1, 1], F32, name="one")
+        nc.vector.memset(one[:], 1.0)
+        seb_ps = psum.tile([P, BANK], F32, name="seb_ps", tag="z0_0")
+        for k in range(CB):
+            nc.tensor.matmul(
+                seb_ps[:, k : k + 1], lhsT=seb_row[:, k * P : (k + 1) * P], rhs=one[:], start=True, stop=True
+            )
+        seb = held.tile([P, CB], F32, name="seb")
+        nc.vector.tensor_copy(seb[:], seb_ps[:, 0:CB])
+
+        z_ps = [[psum.tile([P, BANK], F32, name=f"z{t}_{h}") for h in range(VH)] for t in range(TB)]
+        for k in range(CB):
+            picked = held.tile([P, N], F32, name=f"picked{k}")
+            nc.vector.tensor_tensor(
+                out=picked[:], in0=table_sb[k][:].indirect(offsets[:]), in1=pe_sb[k][:], op=ALU.add
+            )
+            x = held.tile([P, N], BF16, name=f"x{k}")
+            nc.scalar.activation(out=x[:], in_=picked[:], func=ACT.Identity, bias=seb[:, k : k + 1])
+            for t in range(TB):
+                for h in range(VH):
+                    nc.tensor.matmul(
+                        z_ps[t][h][:],
+                        lhsT=x[:, t * P : (t + 1) * P],
+                        rhs=we_sb[k][:, h * BANK : (h + 1) * BANK],
+                        start=(k == 0),
+                        stop=(k == CB - 1),
+                    )
+
+        for t in range(TB):
+            z = rows.tile([P, V], F32, name="z")
+            for h in range(VH):
+                half = slice(h * BANK, (h + 1) * BANK)
+                nc.vector.tensor_tensor(out=z[:, half], in0=z_ps[t][h][:], in1=be_all[:, half], op=ALU.add)
+            neg_max = stats.tile([P, 1], F32, name="neg_max")
+            nc.vector.tensor_reduce(out=neg_max[:], in_=z[:], axis=AXIS.X, op=ALU.max, negate=True)
+            exps = rows.tile([P, V], BF16, name="exps")
+            total = stats.tile([P, 1], F32, name="total")
+            nc.scalar.activation(out=exps[:], in_=z[:], func=ACT.Exp, bias=neg_max[:], accum_out=total[:])
+            log_total = stats.tile([P, 1], F32, name="log_total")
+            nc.scalar.activation(out=log_total[:], in_=total[:], func=ACT.Ln)
+            shift = stats.tile([P, 1], F32, name="shift")
+            nc.vector.tensor_tensor(out=shift[:], in0=log_total[:], in1=neg_max[:], op=ALU.subtract)
+            result = rows.tile([P, V], F32, name="result")
+            nc.vector.tensor_scalar(out=result[:], in0=z[:], scalar1=shift[:], scalar2=None, op0=ALU.subtract)
+            nc.sync.dma_start(out[t * P : (t + 1) * P, :], result[:])

@@ -5,7 +5,6 @@ BF16 = mybir.dt.bfloat16
 U16 = mybir.dt.uint16
 ALU = mybir.AluOpType
 ACT = mybir.ActivationFunctionType
-AXIS = mybir.AxisListType
 
 P = 128
 C, V, N = 768, 1024, 512
@@ -13,6 +12,9 @@ CB = C // P
 TB = N // P
 BANK = 512
 VH = V // BANK
+PARTS = 3
+ROOT = 1024.0
+LAG = 2
 
 FLOPS = 2 * N * C * V
 
@@ -21,68 +23,159 @@ def tile_albertwithsoftmax_kernel(tc, table, pe, se_b, we, be, offs, out):
     nc = tc.nc
     with (
         tc.tile_pool(name="held", bufs=1) as held,
-        tc.tile_pool(name="rows", bufs=2) as rows,
-        tc.tile_pool(name="stats", bufs=4) as stats,
         tc.psum_pool(name="psum", bufs=1) as psum,
     ):
         offsets = held.tile([P, N // 16], U16, name="offsets")
         nc.sync.dma_start(offsets[:], offs)
         seb_row = held.tile([1, C], F32, name="seb_row")
         nc.scalar.dma_start(seb_row[:], se_b.rearrange("c o -> o c"))
-
+        be_rows = held.tile([PARTS, V], F32, name="be_rows")
+        nc.scalar.dma_start(be_rows[:], be.rearrange("o v -> (o v)").partition_broadcast(PARTS))
         table_sb = [held.tile([P, V], F32, name=f"table{k}") for k in range(CB)]
         pe_sb = [held.tile([P, N], F32, name=f"pe{k}") for k in range(CB)]
         we_sb = [held.tile([P, V], BF16, name=f"we{k}") for k in range(CB)]
         for k in range(CB):
             block = slice(k * P, (k + 1) * P)
             nc.sync.dma_start(table_sb[k][:], table[block, :])
-            nc.scalar.dma_start(pe_sb[k][:], pe[block, :])
-            nc.scalar.dma_start(we_sb[k][:], we[block, :])
-        be_all = held.tile([P, V], F32, name="be_all")
-        nc.scalar.dma_start(be_all[:], be.rearrange("o v -> (o v)").partition_broadcast(P))
+            nc.sync.dma_start(pe_sb[k][:], pe[block, :])
+            nc.sync.dma_start(we_sb[k][:], we[block, :])
 
         one = held.tile([1, 1], F32, name="one")
         nc.vector.memset(one[:], 1.0)
+        inv_root = held.tile([P, 1], F32, name="inv_root")
+        nc.vector.memset(inv_root[:], 1.0 / ROOT)
+        ones = held.tile([P, P], BF16, name="ones")
+        nc.gpsimd.memset(ones[:], 1.0)
+        bias_parts = held.tile([P, V], BF16, name="bias_parts")
+        nc.gpsimd.memset(bias_parts[:], 0.0)
+        go_on = held.tile([PARTS, PARTS - 1], F32, name="go_on")
+        nc.gpsimd.memset(go_on[:], -1.0)
+        for r in range(1, PARTS):
+            nc.gpsimd.affine_select(
+                out=go_on[:, r - 1 : r],
+                in_=go_on[:, r - 1 : r],
+                pattern=[[0, 1]],
+                compare_op=ALU.is_ge,
+                fill=0.0,
+                base=-r,
+                channel_multiplier=1,
+            )
+
         seb_ps = psum.tile([P, BANK], F32, name="seb_ps", tag="z0_0")
         for k in range(CB):
             nc.tensor.matmul(
                 seb_ps[:, k : k + 1], lhsT=seb_row[:, k * P : (k + 1) * P], rhs=one[:], start=True, stop=True
             )
         seb = held.tile([P, CB], F32, name="seb")
-        nc.vector.tensor_copy(seb[:], seb_ps[:, 0:CB])
+        nc.scalar.copy(seb[:], seb_ps[:, 0:CB])
 
         z_ps = [[psum.tile([P, BANK], F32, name=f"z{t}_{h}") for h in range(VH)] for t in range(TB)]
-        for k in range(CB):
-            picked = held.tile([P, N], F32, name=f"picked{k}")
-            nc.vector.tensor_tensor(
-                out=picked[:], in0=table_sb[k][:].indirect(offsets[:]), in1=pe_sb[k][:], op=ALU.add
-            )
-            x = held.tile([P, N], BF16, name=f"x{k}")
-            nc.scalar.activation(out=x[:], in_=picked[:], func=ACT.Identity, bias=seb[:, k : k + 1])
-            for t in range(TB):
-                for h in range(VH):
-                    nc.tensor.matmul(
-                        z_ps[t][h][:],
-                        lhsT=x[:, t * P : (t + 1) * P],
-                        rhs=we_sb[k][:, h * BANK : (h + 1) * BANK],
-                        start=(k == 0),
-                        stop=(k == CB - 1),
-                    )
+        picked = [held.tile([P, N], F32, name=f"picked{k}") for k in range(CB)]
+        x = [held.tile([P, N], BF16, name=f"x{k}") for k in range(CB)]
 
+        def look_up(k, t):
+            tokens = slice(t * P, (t + 1) * P)
+            nc.vector.tensor_tensor(
+                out=picked[k][:, tokens],
+                in0=table_sb[k][:].indirect(offsets[:, t * (P // 16) : (t + 1) * (P // 16)]),
+                in1=pe_sb[k][:, tokens],
+                op=ALU.add,
+            )
+            nc.scalar.activation(
+                out=x[k][:, tokens], in_=picked[k][:, tokens], func=ACT.Identity, bias=seb[:, k : k + 1]
+            )
+
+        def multiply(k, t):
+            for h in range(VH):
+                nc.tensor.matmul(
+                    z_ps[t][h][:],
+                    lhsT=x[k][:, t * P : (t + 1) * P],
+                    rhs=we_sb[k][:, h * BANK : (h + 1) * BANK],
+                    start=(k == 0),
+                    stop=(k == CB - 1),
+                )
+
+        left = [be_rows] + [held.tile([PARTS, V], F32, name=f"left{r}") for r in range(1, PARTS)]
+        part = [held.tile([PARTS, V], BF16, name=f"part{r}")[:] for r in range(1, PARTS)] + [bias_parts[0:PARTS, :]]
+
+        def split_bias(step):
+            r = step // 2
+            if step % 2 == 0:
+                nc.scalar.copy(part[r], left[r][:])
+            else:
+                nc.vector.scalar_tensor_tensor(
+                    out=left[r + 1][:], in0=part[r], scalar=go_on[:, r : r + 1], in1=left[r][:], op0=ALU.mult, op1=ALU.add
+                )
+
+        def add_bias(t):
+            for h in range(VH):
+                nc.tensor.matmul(
+                    z_ps[t][h][:],
+                    lhsT=ones[:],
+                    rhs=bias_parts[:, h * BANK : (h + 1) * BANK],
+                    start=False,
+                    stop=False,
+                )
+
+        assert 2 * PARTS - 1 == CB - 1
+        for k in range(CB - 1):
+            for t in range(TB):
+                look_up(k, t)
+                multiply(k, t)
+            split_bias(k)
         for t in range(TB):
-            z = rows.tile([P, V], F32, name="z")
+            look_up(CB - 1, t)
+            add_bias(t)
+            multiply(CB - 1, t)
+
+        neg_z = [held.tile([P, V], F32, name=f"neg_z{t}") for t in range(TB)]
+        neg_max = [[held.tile([P, 1], F32, name=f"neg_max{t}_{h}") for h in range(VH)] for t in range(TB)]
+        root = [held.tile([P, 1], F32, name=f"root{t}") for t in range(TB)]
+        shift = [held.tile([P, 1], F32, name=f"shift{t}") for t in range(TB)]
+
+        def evacuate(t):
+            for h in range(VH):
+                nc.vector.tensor_scalar(
+                    out=neg_z[t][:, h * BANK : (h + 1) * BANK],
+                    in0=z_ps[t][h][:],
+                    scalar1=-1.0,
+                    scalar2=(neg_max[t][h - 1][:] if h > 0 else None),
+                    op0=ALU.mult,
+                    op1=ALU.min,
+                    accum_out=neg_max[t][h][:],
+                )
+
+        def log_sum_exp(t):
+            lowest = neg_max[t][VH - 1]
+            exps = held.tile([P, V], BF16, name=f"exps{t}")
+            total = held.tile([P, 1], F32, name=f"total{t}")
+            nc.scalar.activation(
+                out=exps[:], in_=neg_z[t][:], func=ACT.Exp, bias=lowest[:], scale=-1.0, accum_out=total[:]
+            )
+            nc.gpsimd.tensor_tensor(out=root[t][:], in0=total[:], in1=inv_root[:], op=ALU.pow)
+
+        def finish(t):
+            curve = held.tile([P, 1], F32, name=f"curve{t}")
+            nc.vector.tensor_scalar(out=curve[:], in0=root[t][:], scalar1=-0.5, scalar2=1.5, op0=ALU.mult, op1=ALU.add)
+            slope = held.tile([P, 1], F32, name=f"slope{t}")
+            nc.vector.tensor_scalar(out=slope[:], in0=root[t][:], scalar1=-1.0, scalar2=-ROOT, op0=ALU.add, op1=ALU.mult)
+            nc.vector.tensor_scalar(
+                out=shift[t][:], in0=curve[:], scalar1=slope[:], scalar2=neg_max[t][VH - 1][:], op0=ALU.mult, op1=ALU.add
+            )
+            result = held.tile([P, V], F32, name=f"result{t}")
+            nc.vector.tensor_scalar(
+                out=result[:, 0:BANK], in0=neg_z[t][:, 0:BANK], scalar1=-1.0, scalar2=shift[t][:], op0=ALU.mult, op1=ALU.add
+            )
+            nc.scalar.activation(
+                out=result[:, BANK:V], in_=neg_z[t][:, BANK:V], func=ACT.Identity, bias=shift[t][:], scale=-1.0
+            )
             for h in range(VH):
                 half = slice(h * BANK, (h + 1) * BANK)
-                nc.vector.tensor_tensor(out=z[:, half], in0=z_ps[t][h][:], in1=be_all[:, half], op=ALU.add)
-            neg_max = stats.tile([P, 1], F32, name="neg_max")
-            nc.vector.tensor_reduce(out=neg_max[:], in_=z[:], axis=AXIS.X, op=ALU.max, negate=True)
-            exps = rows.tile([P, V], BF16, name="exps")
-            total = stats.tile([P, 1], F32, name="total")
-            nc.scalar.activation(out=exps[:], in_=z[:], func=ACT.Exp, bias=neg_max[:], accum_out=total[:])
-            log_total = stats.tile([P, 1], F32, name="log_total")
-            nc.scalar.activation(out=log_total[:], in_=total[:], func=ACT.Ln)
-            shift = stats.tile([P, 1], F32, name="shift")
-            nc.vector.tensor_tensor(out=shift[:], in0=log_total[:], in1=neg_max[:], op=ALU.subtract)
-            result = rows.tile([P, V], F32, name="result")
-            nc.vector.tensor_scalar(out=result[:], in0=z[:], scalar1=shift[:], scalar2=None, op0=ALU.subtract)
-            nc.sync.dma_start(out[t * P : (t + 1) * P, :], result[:])
+                nc.sync.dma_start(out[t * P : (t + 1) * P, half], result[:, half])
+
+        for step in range(TB + LAG):
+            if step < TB:
+                evacuate(step)
+                log_sum_exp(step)
+            if step >= LAG:
+                finish(step - LAG)

@@ -15,6 +15,7 @@ VH = V // BANK
 PARTS = 3
 ROOT = 1024.0
 LAG = 2
+WARM = 4
 
 FLOPS = 2 * N * C * V
 
@@ -69,6 +70,10 @@ def tile_albertwithsoftmax_kernel(tc, table, pe, se_b, we, be, offs, out):
         seb = held.tile([P, CB], F32, name="seb")
         nc.scalar.copy(seb[:], seb_ps[:, 0:CB])
 
+        warm_ps = psum.tile([P, BANK], F32, name="warm_ps", tag=f"z{TB - 1}_{VH - 1}")
+        for i in range(WARM):
+            nc.tensor.matmul(warm_ps[:], lhsT=ones[:], rhs=bias_parts[:, 0:BANK], start=True, stop=True)
+
         z_ps = [[psum.tile([P, BANK], F32, name=f"z{t}_{h}") for h in range(VH)] for t in range(TB)]
         picked = [held.tile([P, N], F32, name=f"picked{k}") for k in range(CB)]
         x = [held.tile([P, N], BF16, name=f"x{k}") for k in range(CB)]
@@ -85,15 +90,14 @@ def tile_albertwithsoftmax_kernel(tc, table, pe, se_b, we, be, offs, out):
                 out=x[k][:, tokens], in_=picked[k][:, tokens], func=ACT.Identity, bias=seb[:, k : k + 1]
             )
 
-        def multiply(k, t):
-            for h in range(VH):
-                nc.tensor.matmul(
-                    z_ps[t][h][:],
-                    lhsT=x[k][:, t * P : (t + 1) * P],
-                    rhs=we_sb[k][:, h * BANK : (h + 1) * BANK],
-                    start=(k == 0),
-                    stop=(k == CB - 1),
-                )
+        def multiply(k, t, h):
+            nc.tensor.matmul(
+                z_ps[t][h][:],
+                lhsT=x[k][:, t * P : (t + 1) * P],
+                rhs=we_sb[k][:, h * BANK : (h + 1) * BANK],
+                start=(k == 0),
+                stop=(k == CB - 1),
+            )
 
         left = [be_rows] + [held.tile([PARTS, V], F32, name=f"left{r}") for r in range(1, PARTS)]
         part = [held.tile([PARTS, V], BF16, name=f"part{r}")[:] for r in range(1, PARTS)] + [bias_parts[0:PARTS, :]]
@@ -107,26 +111,23 @@ def tile_albertwithsoftmax_kernel(tc, table, pe, se_b, we, be, offs, out):
                     out=left[r + 1][:], in0=part[r], scalar=go_on[:, r : r + 1], in1=left[r][:], op0=ALU.mult, op1=ALU.add
                 )
 
-        def add_bias(t):
-            for h in range(VH):
-                nc.tensor.matmul(
-                    z_ps[t][h][:],
-                    lhsT=ones[:],
-                    rhs=bias_parts[:, h * BANK : (h + 1) * BANK],
-                    start=False,
-                    stop=False,
-                )
+        def add_bias(t, h):
+            nc.tensor.matmul(
+                z_ps[t][h][:], lhsT=ones[:], rhs=bias_parts[:, h * BANK : (h + 1) * BANK], start=False, stop=False
+            )
 
         assert 2 * PARTS - 1 == CB - 1
         for k in range(CB - 1):
             for t in range(TB):
                 look_up(k, t)
-                multiply(k, t)
+                for h in range(VH):
+                    multiply(k, t, h)
             split_bias(k)
         for t in range(TB):
             look_up(CB - 1, t)
-            add_bias(t)
-            multiply(CB - 1, t)
+            for h in range(VH):
+                add_bias(t, h)
+                multiply(CB - 1, t, h)
 
         neg_z = [held.tile([P, V], F32, name=f"neg_z{t}") for t in range(TB)]
         neg_max = [[held.tile([P, 1], F32, name=f"neg_max{t}_{h}") for h in range(VH)] for t in range(TB)]

@@ -14,7 +14,9 @@ BANK = 512
 VH = V // BANK
 PARTS = 3
 ROOT = 1024.0
-LAG = 2
+LAG = 1
+LAST = 2
+RING = 3
 WARM = 4
 
 FLOPS = 2 * N * C * V
@@ -24,6 +26,7 @@ def tile_albertwithsoftmax_kernel(tc, table, pe, se_b, we, be, offs, out):
     nc = tc.nc
     with (
         tc.tile_pool(name="held", bufs=1) as held,
+        tc.tile_pool(name="ring", bufs=RING) as ring,
         tc.psum_pool(name="psum", bufs=1) as psum,
     ):
         offsets = held.tile([P, N // 16], U16, name="offsets")
@@ -76,7 +79,7 @@ def tile_albertwithsoftmax_kernel(tc, table, pe, se_b, we, be, offs, out):
 
         z_ps = [[psum.tile([P, BANK], F32, name=f"z{t}_{h}") for h in range(VH)] for t in range(TB)]
         picked = [held.tile([P, N], F32, name=f"picked{k}") for k in range(CB)]
-        x = [held.tile([P, N], BF16, name=f"x{k}") for k in range(CB)]
+        x = [held.tile([P, N], BF16, name=f"x{k}") for k in range(CB - LAST)]
 
         def look_up(k, t):
             tokens = slice(t * P, (t + 1) * P)
@@ -86,17 +89,15 @@ def tile_albertwithsoftmax_kernel(tc, table, pe, se_b, we, be, offs, out):
                 in1=pe_sb[k][:, tokens],
                 op=ALU.add,
             )
+
+        def round_off(k, t, x_kt):
             nc.scalar.activation(
-                out=x[k][:, tokens], in_=picked[k][:, tokens], func=ACT.Identity, bias=seb[:, k : k + 1]
+                out=x_kt, in_=picked[k][:, t * P : (t + 1) * P], func=ACT.Identity, bias=seb[:, k : k + 1]
             )
 
-        def multiply(k, t, h):
+        def multiply(k, t, h, x_kt):
             nc.tensor.matmul(
-                z_ps[t][h][:],
-                lhsT=x[k][:, t * P : (t + 1) * P],
-                rhs=we_sb[k][:, h * BANK : (h + 1) * BANK],
-                start=(k == 0),
-                stop=(k == CB - 1),
+                z_ps[t][h][:], lhsT=x_kt, rhs=we_sb[k][:, h * BANK : (h + 1) * BANK], start=(k == 0), stop=False
             )
 
         left = [be_rows] + [held.tile([PARTS, V], F32, name=f"left{r}") for r in range(1, PARTS)]
@@ -113,21 +114,41 @@ def tile_albertwithsoftmax_kernel(tc, table, pe, se_b, we, be, offs, out):
 
         def add_bias(t, h):
             nc.tensor.matmul(
-                z_ps[t][h][:], lhsT=ones[:], rhs=bias_parts[:, h * BANK : (h + 1) * BANK], start=False, stop=False
+                z_ps[t][h][:], lhsT=ones[:], rhs=bias_parts[:, h * BANK : (h + 1) * BANK], start=False, stop=True
             )
 
-        assert 2 * PARTS - 1 == CB - 1
-        for k in range(CB - 1):
+        steps = 2 * PARTS - 1
+        early = CB - LAST
+        steps_a_block = (steps + early - 1) // early
+        for k in range(early):
+            for t in range(TB):
+                x_kt = x[k][:, t * P : (t + 1) * P]
+                look_up(k, t)
+                round_off(k, t, x_kt)
+                for h in range(VH):
+                    multiply(k, t, h, x_kt)
+            for step in range(k * steps_a_block, min((k + 1) * steps_a_block, steps)):
+                split_bias(step)
+        for k in range(early, CB):
             for t in range(TB):
                 look_up(k, t)
-                for h in range(VH):
-                    multiply(k, t, h)
-            split_bias(k)
-        for t in range(TB):
-            look_up(CB - 1, t)
+
+        def complete(t):
+            late = {}
+            for k in range(early, CB):
+                late[k] = ring.tile([P, P], BF16, name="x_late")
+                nc.gpsimd.tensor_scalar(
+                    out=late[k][:],
+                    in0=picked[k][:, t * P : (t + 1) * P],
+                    scalar1=seb[:, k : k + 1],
+                    scalar2=1.0,
+                    op0=ALU.add,
+                    op1=ALU.mult,
+                )
             for h in range(VH):
+                for k in range(early, CB):
+                    multiply(k, t, h, late[k][:])
                 add_bias(t, h)
-                multiply(CB - 1, t, h)
 
         neg_z = [held.tile([P, V], F32, name=f"neg_z{t}") for t in range(TB)]
         neg_max = [[held.tile([P, 1], F32, name=f"neg_max{t}_{h}") for h in range(VH)] for t in range(TB)]
@@ -176,6 +197,7 @@ def tile_albertwithsoftmax_kernel(tc, table, pe, se_b, we, be, offs, out):
 
         for step in range(TB + LAG):
             if step < TB:
+                complete(step)
                 evacuate(step)
                 log_sum_exp(step)
             if step >= LAG:

@@ -17,7 +17,6 @@ ROOT = 1024.0
 LAG = 1
 LAST = 2
 RING = 3
-WARM = 4
 
 FLOPS = 2 * N * C * V
 
@@ -29,23 +28,28 @@ def tile_albertwithsoftmax_kernel(tc, table, pe, se_b, we, be, offs, out):
         tc.tile_pool(name="ring", bufs=RING) as ring,
         tc.psum_pool(name="psum", bufs=1) as psum,
     ):
-        offsets = held.tile([P, N // 16], U16, name="offsets")
-        nc.sync.dma_start(offsets[:], offs)
-        seb_row = held.tile([1, C], F32, name="seb_row")
-        nc.scalar.dma_start(seb_row[:], se_b.rearrange("c o -> o c"))
-        be_rows = held.tile([PARTS, V], F32, name="be_rows")
-        nc.scalar.dma_start(be_rows[:], be.rearrange("o v -> (o v)").partition_broadcast(PARTS))
+        table_by = table.rearrange("(p k) v -> p k v", k=CB)
+        pe_by = pe.rearrange("(p k) n -> p k n", k=CB)
+        we_by = we.rearrange("(p k) v -> p k v", k=CB)
         table_sb = [held.tile([P, V], F32, name=f"table{k}") for k in range(CB)]
         pe_sb = [held.tile([P, N], F32, name=f"pe{k}") for k in range(CB)]
         we_sb = [held.tile([P, V], BF16, name=f"we{k}") for k in range(CB)]
-        for k in range(CB):
-            block = slice(k * P, (k + 1) * P)
-            nc.sync.dma_start(table_sb[k][:], table[block, :])
-            nc.sync.dma_start(pe_sb[k][:], pe[block, :])
-            nc.sync.dma_start(we_sb[k][:], we[block, :])
+        offsets = held.tile([P, N // 16], U16, name="offsets")
+        seb = held.tile([P, CB], F32, name="seb")
+        be_rows = held.tile([PARTS, V], F32, name="be_rows")
+        nc.sync.dma_start(table_sb[0][:], table_by[:, 0, :])
+        nc.sync.dma_start(offsets[:], offs)
+        nc.scalar.dma_start(seb[:], se_b.rearrange("(p k) o -> p (k o)", k=CB))
+        nc.scalar.dma_start(pe_sb[0][:, 0:P], pe_by[:, 0, 0:P])
+        nc.scalar.dma_start(be_rows[:], be.rearrange("o v -> (o v)").partition_broadcast(PARTS))
+        nc.sync.dma_start(we_sb[0][:, 0:BANK], we_by[:, 0, 0:BANK])
+        nc.sync.dma_start(we_sb[0][:, BANK:V], we_by[:, 0, BANK:V])
+        nc.sync.dma_start(pe_sb[0][:, P:N], pe_by[:, 0, P:N])
+        for k in range(1, CB):
+            nc.sync.dma_start(table_sb[k][:], table_by[:, k, :])
+            nc.sync.dma_start(pe_sb[k][:], pe_by[:, k, :])
+            nc.sync.dma_start(we_sb[k][:], we_by[:, k, :])
 
-        one = held.tile([1, 1], F32, name="one")
-        nc.vector.memset(one[:], 1.0)
         inv_root = held.tile([P, 1], F32, name="inv_root")
         nc.vector.memset(inv_root[:], 1.0 / ROOT)
         ones = held.tile([P, P], BF16, name="ones")
@@ -64,18 +68,6 @@ def tile_albertwithsoftmax_kernel(tc, table, pe, se_b, we, be, offs, out):
                 base=-r,
                 channel_multiplier=1,
             )
-
-        seb_ps = psum.tile([P, BANK], F32, name="seb_ps", tag="z0_0")
-        for k in range(CB):
-            nc.tensor.matmul(
-                seb_ps[:, k : k + 1], lhsT=seb_row[:, k * P : (k + 1) * P], rhs=one[:], start=True, stop=True
-            )
-        seb = held.tile([P, CB], F32, name="seb")
-        nc.scalar.copy(seb[:], seb_ps[:, 0:CB])
-
-        warm_ps = psum.tile([P, BANK], F32, name="warm_ps", tag=f"z{TB - 1}_{VH - 1}")
-        for i in range(WARM):
-            nc.tensor.matmul(warm_ps[:], lhsT=ones[:], rhs=bias_parts[:, 0:BANK], start=True, stop=True)
 
         z_ps = [[psum.tile([P, BANK], F32, name=f"z{t}_{h}") for h in range(VH)] for t in range(TB)]
         picked = [held.tile([P, N], F32, name=f"picked{k}") for k in range(CB)]

@@ -89,7 +89,7 @@ def tile_albertwithsoftmax_kernel(tc, table, pe, se_b, we, be, offs, out):
 
         def multiply(k, t, h, x_kt):
             nc.tensor.matmul(
-                z_ps[t][h][:], lhsT=x_kt, rhs=we_sb[k][:, h * BANK : (h + 1) * BANK], start=(k == 0), stop=False
+                z_ps[t][h][:], lhsT=x_kt, rhs=we_sb[k][:, h * BANK : (h + 1) * BANK], start=(k == 0), stop=(k == CB - 1)
             )
 
         left = [be_rows] + [held.tile([PARTS, V], F32, name=f"left{r}") for r in range(1, PARTS)]
@@ -106,7 +106,7 @@ def tile_albertwithsoftmax_kernel(tc, table, pe, se_b, we, be, offs, out):
 
         def add_bias(t, h):
             nc.tensor.matmul(
-                z_ps[t][h][:], lhsT=ones[:], rhs=bias_parts[:, h * BANK : (h + 1) * BANK], start=False, stop=True
+                z_ps[t][h][:], lhsT=ones[:], rhs=bias_parts[:, h * BANK : (h + 1) * BANK], start=False, stop=False
             )
 
         steps = 2 * PARTS - 1
@@ -138,9 +138,10 @@ def tile_albertwithsoftmax_kernel(tc, table, pe, se_b, we, be, offs, out):
                     op1=ALU.mult,
                 )
             for h in range(VH):
-                for k in range(early, CB):
+                for k in range(early, CB - 1):
                     multiply(k, t, h, late[k][:])
                 add_bias(t, h)
+                multiply(CB - 1, t, h, late[CB - 1][:])
 
         neg_z = [held.tile([P, V], F32, name=f"neg_z{t}") for t in range(TB)]
         neg_max = [[held.tile([P, 1], F32, name=f"neg_max{t}_{h}") for h in range(VH)] for t in range(TB)]

@@ -42,8 +42,7 @@ def tile_albertwithsoftmax_kernel(tc, table, pe, se_b, we, be, offs, out):
         nc.scalar.dma_start(seb[:], se_b.rearrange("(p k) o -> p (k o)", k=CB))
         nc.scalar.dma_start(pe_sb[0][:, 0:P], pe_by[:, 0, 0:P])
         nc.scalar.dma_start(be_rows[:], be.rearrange("o v -> (o v)").partition_broadcast(PARTS))
-        nc.sync.dma_start(we_sb[0][:, 0:BANK], we_by[:, 0, 0:BANK])
-        nc.sync.dma_start(we_sb[0][:, BANK:V], we_by[:, 0, BANK:V])
+        nc.sync.dma_start(we_sb[0][:], we_by[:, 0, :])
         nc.sync.dma_start(pe_sb[0][:, P:N], pe_by[:, 0, P:N])
         for k in range(1, CB):
             nc.sync.dma_start(table_sb[k][:], table_by[:, k, :])

@@ -16,7 +16,7 @@ PARTS = 3
 ROOT = 1024.0
 LAG = 1
 LAST = 2
-RING = 3
+RING = 2 * LAST + 1
 
 FLOPS = 2 * N * C * V
 
@@ -44,9 +44,14 @@ def tile_albertwithsoftmax_kernel(tc, table, pe, se_b, we, be, offs, out):
         nc.scalar.dma_start(be_rows[:], be.rearrange("o v -> (o v)").partition_broadcast(PARTS))
         nc.sync.dma_start(we_sb[0][:], we_by[:, 0, :])
         nc.sync.dma_start(pe_sb[0][:, P:N], pe_by[:, 0, P:N])
-        for k in range(1, CB):
+        for k in range(1, CB - LAST):
             nc.sync.dma_start(table_sb[k][:], table_by[:, k, :])
             nc.sync.dma_start(pe_sb[k][:], pe_by[:, k, :])
+            nc.sync.dma_start(we_sb[k][:], we_by[:, k, :])
+        for k in range(CB - LAST, CB):
+            nc.sync.dma_start(table_sb[k][:], table_by[:, k, :])
+            nc.sync.dma_start(pe_sb[k][:], pe_by[:, k, :])
+        for k in range(CB - LAST, CB):
             nc.sync.dma_start(we_sb[k][:], we_by[:, k, :])
 
         inv_root = held.tile([P, 1], F32, name="inv_root")
@@ -128,14 +133,7 @@ def tile_albertwithsoftmax_kernel(tc, table, pe, se_b, we, be, offs, out):
             late = {}
             for k in range(early, CB):
                 late[k] = ring.tile([P, P], BF16, name="x_late")
-                nc.gpsimd.tensor_scalar(
-                    out=late[k][:],
-                    in0=picked[k][:, t * P : (t + 1) * P],
-                    scalar1=seb[:, k : k + 1],
-                    scalar2=1.0,
-                    op0=ALU.add,
-                    op1=ALU.mult,
-                )
+                round_off(k, t, late[k][:])
             for h in range(VH):
                 for k in range(early, CB - 1):
                     multiply(k, t, h, late[k][:])

@@ -12,6 +12,7 @@ CB = C // P
 TB = N // P
 BANK = 512
 VH = V // BANK
+VP = V // P
 PARTS = 3
 ROOT = 1024.0
 LAG = 1
@@ -36,31 +37,42 @@ def tile_albertwithsoftmax_kernel(tc, table, pe, se_b, we, be, offs, out):
         we_sb = [held.tile([P, V], BF16, name=f"we{k}") for k in range(CB)]
         offsets = held.tile([P, N // 16], U16, name="offsets")
         seb = held.tile([P, CB], F32, name="seb")
-        be_rows = held.tile([PARTS, V], F32, name="be_rows")
+        be_rows = held.tile([PARTS * VP, P], F32, name="be_rows")
         nc.sync.dma_start(table_sb[0][:], table_by[:, 0, :])
         nc.sync.dma_start(offsets[:], offs)
         nc.scalar.dma_start(seb[:], se_b.rearrange("(p k) o -> p (k o)", k=CB))
         nc.scalar.dma_start(pe_sb[0][:, 0:P], pe_by[:, 0, 0:P])
-        nc.scalar.dma_start(be_rows[:], be.rearrange("o v -> (o v)").partition_broadcast(PARTS))
         nc.sync.dma_start(we_sb[0][:], we_by[:, 0, :])
         nc.sync.dma_start(pe_sb[0][:, P:N], pe_by[:, 0, P:N])
-        for k in range(1, CB - LAST):
+        for k in range(1, CB):
             nc.sync.dma_start(table_sb[k][:], table_by[:, k, :])
             nc.sync.dma_start(pe_sb[k][:], pe_by[:, k, :])
-            nc.sync.dma_start(we_sb[k][:], we_by[:, k, :])
-        for k in range(CB - LAST, CB):
-            nc.sync.dma_start(table_sb[k][:], table_by[:, k, :])
-            nc.sync.dma_start(pe_sb[k][:], pe_by[:, k, :])
-        for k in range(CB - LAST, CB):
-            nc.sync.dma_start(we_sb[k][:], we_by[:, k, :])
+            if k > 1:
+                nc.sync.dma_start(we_sb[k - 1][:], we_by[:, k - 1, :])
+            if k == 1:
+                for r in range(PARTS):
+                    nc.sync.dma_start(be_rows[r * VP : (r + 1) * VP, :], be.rearrange("o (c w) -> (o c) w", w=P))
+        nc.sync.dma_start(we_sb[CB - 1][:], we_by[:, CB - 1, :])
 
         inv_root = held.tile([P, 1], F32, name="inv_root")
         nc.vector.memset(inv_root[:], 1.0 / ROOT)
-        ones = held.tile([P, P], BF16, name="ones")
-        nc.gpsimd.memset(ones[:], 1.0)
-        bias_parts = held.tile([P, V], BF16, name="bias_parts")
+        one = held.tile([P, 1], F32, name="one")
+        nc.scalar.activation(out=one[:], in_=inv_root[:], func=ACT.Exp, scale=0.0)
+        bias_parts = held.tile([P, P], BF16, name="bias_parts")
         nc.gpsimd.memset(bias_parts[:], 0.0)
-        go_on = held.tile([PARTS, PARTS - 1], F32, name="go_on")
+        pick = held.tile([P, VP], BF16, name="pick")
+        nc.gpsimd.memset(pick[:], 0.0)
+        for r in range(PARTS):
+            nc.gpsimd.affine_select(
+                out=pick[:],
+                in_=pick[:],
+                pattern=[[-1, VP]],
+                compare_op=ALU.not_equal,
+                fill=1.0,
+                base=-r * VP,
+                channel_multiplier=1,
+            )
+        go_on = held.tile([PARTS * VP, PARTS - 1], F32, name="go_on")
         nc.gpsimd.memset(go_on[:], -1.0)
         for r in range(1, PARTS):
             nc.gpsimd.affine_select(
@@ -69,7 +81,7 @@ def tile_albertwithsoftmax_kernel(tc, table, pe, se_b, we, be, offs, out):
                 pattern=[[0, 1]],
                 compare_op=ALU.is_ge,
                 fill=0.0,
-                base=-r,
+                base=-r * VP,
                 channel_multiplier=1,
             )
 
@@ -96,26 +108,35 @@ def tile_albertwithsoftmax_kernel(tc, table, pe, se_b, we, be, offs, out):
                 z_ps[t][h][:], lhsT=x_kt, rhs=we_sb[k][:, h * BANK : (h + 1) * BANK], start=(k == 0), stop=(k == CB - 1)
             )
 
-        left = [be_rows] + [held.tile([PARTS, V], F32, name=f"left{r}") for r in range(1, PARTS)]
-        part = [held.tile([PARTS, V], BF16, name=f"part{r}")[:] for r in range(1, PARTS)] + [bias_parts[0:PARTS, :]]
+        rows = PARTS * VP
+        left = [be_rows] + [held.tile([rows, P], F32, name=f"left{r}") for r in range(1, PARTS)]
+        part = [held.tile([rows, P], BF16, name=f"part{r}")[:] for r in range(1, PARTS)] + [bias_parts[0:rows, :]]
 
-        def split_bias(step):
-            r = step // 2
-            if step % 2 == 0:
+        def split_bias():
+            for r in range(PARTS):
                 nc.scalar.copy(part[r], left[r][:])
-            else:
-                nc.vector.scalar_tensor_tensor(
-                    out=left[r + 1][:], in0=part[r], scalar=go_on[:, r : r + 1], in1=left[r][:], op0=ALU.mult, op1=ALU.add
-                )
+                if r < PARTS - 1:
+                    nc.vector.scalar_tensor_tensor(
+                        out=left[r + 1][:],
+                        in0=part[r],
+                        scalar=go_on[:, r : r + 1],
+                        in1=left[r][:],
+                        op0=ALU.mult,
+                        op1=ALU.add,
+                    )
 
         def add_bias(t, h):
-            nc.tensor.matmul(
-                z_ps[t][h][:], lhsT=ones[:], rhs=bias_parts[:, h * BANK : (h + 1) * BANK], start=False, stop=False
-            )
+            for i in range(BANK // P):
+                c = h * (BANK // P) + i
+                nc.tensor.matmul(
+                    z_ps[t][h][:, i * P : (i + 1) * P],
+                    lhsT=pick[:, c : c + 1].to_broadcast([P, P]),
+                    rhs=bias_parts[:],
+                    start=False,
+                    stop=False,
+                )
 
-        steps = 2 * PARTS - 1
         early = CB - LAST
-        steps_a_block = (steps + early - 1) // early
         for k in range(early):
             for t in range(TB):
                 x_kt = x[k][:, t * P : (t + 1) * P]
@@ -123,8 +144,8 @@ def tile_albertwithsoftmax_kernel(tc, table, pe, se_b, we, be, offs, out):
                 round_off(k, t, x_kt)
                 for h in range(VH):
                     multiply(k, t, h, x_kt)
-            for step in range(k * steps_a_block, min((k + 1) * steps_a_block, steps)):
-                split_bias(step)
+            if k == 1:
+                split_bias()
         for k in range(early, CB):
             for t in range(TB):
                 look_up(k, t)

@@ -146,6 +146,9 @@ def tile_albertwithsoftmax_kernel(tc, table, pe, se_b, we, be, offs, out):
                     multiply(k, t, h, x_kt)
             if k == 1:
                 split_bias()
+                for t in range(TB // 2):
+                    for h in range(VH):
+                        add_bias(t, h)
         for k in range(early, CB):
             for t in range(TB):
                 look_up(k, t)
@@ -158,7 +161,8 @@ def tile_albertwithsoftmax_kernel(tc, table, pe, se_b, we, be, offs, out):
             for h in range(VH):
                 for k in range(early, CB - 1):
                     multiply(k, t, h, late[k][:])
-                add_bias(t, h)
+                if t >= TB // 2:
+                    add_bias(t, h)
                 multiply(CB - 1, t, h, late[CB - 1][:])
 
         neg_z = [held.tile([P, V], F32, name=f"neg_z{t}") for t in range(TB)]

import concourse.mybir as mybir

F32 = mybir.dt.float32
BF16 = mybir.dt.bfloat16
U16 = mybir.dt.uint16
ALU = mybir.AluOpType
ACT = mybir.ActivationFunctionType

P = 128
C, V, N = 768, 1024, 512
CB = C // P
TB = N // P
BANK = 512
VH = V // BANK
VP = V // P
PARTS = 3
ROOT = 1024.0
LAG = 1
LAST = 2
RING = 2 * LAST + 1

FLOPS = 2 * N * C * V


def tile_albertwithsoftmax_kernel(tc, table, pe, se_b, we, be, offs, out):
    nc = tc.nc
    with (
        tc.tile_pool(name="held", bufs=1) as held,
        tc.tile_pool(name="ring", bufs=RING) as ring,
        tc.psum_pool(name="psum", bufs=1) as psum,
    ):
        table_by = table.rearrange("(p k) v -> p k v", k=CB)
        pe_by = pe.rearrange("(p k) n -> p k n", k=CB)
        we_by = we.rearrange("(p k) v -> p k v", k=CB)
        table_sb = [held.tile([P, V], F32, name=f"table{k}") for k in range(CB)]
        pe_sb = [held.tile([P, N], F32, name=f"pe{k}") for k in range(CB)]
        we_sb = [held.tile([P, V], BF16, name=f"we{k}") for k in range(CB)]
        offsets = held.tile([P, N // 16], U16, name="offsets")
        seb = held.tile([P, CB], F32, name="seb")
        be_rows = held.tile([PARTS * VP, P], F32, name="be_rows")
        nc.sync.dma_start(table_sb[0][:], table_by[:, 0, :])
        nc.sync.dma_start(offsets[:], offs)
        nc.scalar.dma_start(seb[:], se_b.rearrange("(p k) o -> p (k o)", k=CB))
        nc.scalar.dma_start(pe_sb[0][:, 0:P], pe_by[:, 0, 0:P])
        nc.sync.dma_start(we_sb[0][:], we_by[:, 0, :])
        nc.sync.dma_start(pe_sb[0][:, P:N], pe_by[:, 0, P:N])
        for k in range(1, CB):
            nc.sync.dma_start(table_sb[k][:], table_by[:, k, :])
            nc.sync.dma_start(pe_sb[k][:], pe_by[:, k, :])
            if k > 1:
                nc.sync.dma_start(we_sb[k - 1][:], we_by[:, k - 1, :])
            if k == 1:
                for r in range(PARTS):
                    nc.sync.dma_start(be_rows[r * VP : (r + 1) * VP, :], be.rearrange("o (c w) -> (o c) w", w=P))
        nc.sync.dma_start(we_sb[CB - 1][:], we_by[:, CB - 1, :])

        inv_root = held.tile([P, 1], F32, name="inv_root")
        nc.vector.memset(inv_root[:], 1.0 / ROOT)
        one = held.tile([P, 1], F32, name="one")
        nc.scalar.activation(out=one[:], in_=inv_root[:], func=ACT.Exp, scale=0.0)
        bias_parts = held.tile([P, P], BF16, name="bias_parts")
        nc.gpsimd.memset(bias_parts[:], 0.0)
        pick = held.tile([P, VP], BF16, name="pick")
        nc.gpsimd.memset(pick[:], 0.0)
        for r in range(PARTS):
            nc.gpsimd.affine_select(
                out=pick[:],
                in_=pick[:],
                pattern=[[-1, VP]],
                compare_op=ALU.not_equal,
                fill=1.0,
                base=-r * VP,
                channel_multiplier=1,
            )
        go_on = held.tile([PARTS * VP, PARTS - 1], F32, name="go_on")
        nc.gpsimd.memset(go_on[:], -1.0)
        for r in range(1, PARTS):
            nc.gpsimd.affine_select(
                out=go_on[:, r - 1 : r],
                in_=go_on[:, r - 1 : r],
                pattern=[[0, 1]],
                compare_op=ALU.is_ge,
                fill=0.0,
                base=-r * VP,
                channel_multiplier=1,
            )

        z_ps = [[psum.tile([P, BANK], F32, name=f"z{t}_{h}") for h in range(VH)] for t in range(TB)]
        picked = [held.tile([P, N], F32, name=f"picked{k}") for k in range(CB)]
        x = [held.tile([P, N], BF16, name=f"x{k}") for k in range(CB - LAST)]

        def look_up(k, t):
            tokens = slice(t * P, (t + 1) * P)
            nc.vector.tensor_tensor(
                out=picked[k][:, tokens],
                in0=table_sb[k][:].indirect(offsets[:, t * (P // 16) : (t + 1) * (P // 16)]),
                in1=pe_sb[k][:, tokens],
                op=ALU.add,
            )

        def round_off(k, t, x_kt):
            nc.scalar.activation(
                out=x_kt, in_=picked[k][:, t * P : (t + 1) * P], func=ACT.Identity, bias=seb[:, k : k + 1]
            )

        def multiply(k, t, h, x_kt):
            nc.tensor.matmul(
                z_ps[t][h][:], lhsT=x_kt, rhs=we_sb[k][:, h * BANK : (h + 1) * BANK], start=(k == 0), stop=(k == CB - 1)
            )

        rows = PARTS * VP
        left = [be_rows] + [held.tile([rows, P], F32, name=f"left{r}") for r in range(1, PARTS)]
        part = [held.tile([rows, P], BF16, name=f"part{r}")[:] for r in range(1, PARTS)] + [bias_parts[0:rows, :]]

        def split_bias():
            for r in range(PARTS):
                nc.scalar.copy(part[r], left[r][:])
                if r < PARTS - 1:
                    nc.vector.scalar_tensor_tensor(
                        out=left[r + 1][:],
                        in0=part[r],
                        scalar=go_on[:, r : r + 1],
                        in1=left[r][:],
                        op0=ALU.mult,
                        op1=ALU.add,
                    )

        def add_bias(t, h):
            for i in range(BANK // P):
                c = h * (BANK // P) + i
                nc.tensor.matmul(
                    z_ps[t][h][:, i * P : (i + 1) * P],
                    lhsT=pick[:, c : c + 1].to_broadcast([P, P]),
                    rhs=bias_parts[:],
                    start=False,
                    stop=False,
                )

        early = CB - LAST
        for k in range(early):
            for t in range(TB):
                x_kt = x[k][:, t * P : (t + 1) * P]
                look_up(k, t)
                round_off(k, t, x_kt)
                for h in range(VH):
                    multiply(k, t, h, x_kt)
            if k == 1:
                split_bias()
                for t in range(TB // 2):
                    for h in range(VH):
                        add_bias(t, h)
        for k in range(early, CB):
            for t in range(TB):
                look_up(k, t)

        def complete(t):
            late = {}
            for k in range(early, CB):
                late[k] = ring.tile([P, P], BF16, name="x_late")
                round_off(k, t, late[k][:])
            for h in range(VH):
                for k in range(early, CB - 1):
                    multiply(k, t, h, late[k][:])
                if t >= TB // 2:
                    add_bias(t, h)
                multiply(CB - 1, t, h, late[CB - 1][:])

        neg_z = [held.tile([P, V], F32, name=f"neg_z{t}") for t in range(TB)]
        neg_max = [[held.tile([P, 1], F32, name=f"neg_max{t}_{h}") for h in range(VH)] for t in range(TB)]
        root = [held.tile([P, 1], F32, name=f"root{t}") for t in range(TB)]
        shift = [held.tile([P, 1], F32, name=f"shift{t}") for t in range(TB)]

        def evacuate(t):
            for h in range(VH):
                nc.vector.tensor_scalar(
                    out=neg_z[t][:, h * BANK : (h + 1) * BANK],
                    in0=z_ps[t][h][:],
                    scalar1=-1.0,
                    scalar2=(neg_max[t][h - 1][:] if h > 0 else None),
                    op0=ALU.mult,
                    op1=ALU.min,
                    accum_out=neg_max[t][h][:],
                )

        def log_sum_exp(t):
            lowest = neg_max[t][VH - 1]
            exps = held.tile([P, V], BF16, name=f"exps{t}")
            total = held.tile([P, 1], F32, name=f"total{t}")
            nc.scalar.activation(
                out=exps[:], in_=neg_z[t][:], func=ACT.Exp, bias=lowest[:], scale=-1.0, accum_out=total[:]
            )
            nc.gpsimd.tensor_tensor(out=root[t][:], in0=total[:], in1=inv_root[:], op=ALU.pow)

        def finish(t):
            curve = held.tile([P, 1], F32, name=f"curve{t}")
            nc.vector.tensor_scalar(out=curve[:], in0=root[t][:], scalar1=-0.5, scalar2=1.5, op0=ALU.mult, op1=ALU.add)
            slope = held.tile([P, 1], F32, name=f"slope{t}")
            nc.vector.tensor_scalar(out=slope[:], in0=root[t][:], scalar1=-1.0, scalar2=-ROOT, op0=ALU.add, op1=ALU.mult)
            nc.vector.tensor_scalar(
                out=shift[t][:], in0=curve[:], scalar1=slope[:], scalar2=neg_max[t][VH - 1][:], op0=ALU.mult, op1=ALU.add
            )
            result = held.tile([P, V], F32, name=f"result{t}")
            nc.vector.tensor_scalar(
                out=result[:, 0:BANK], in0=neg_z[t][:, 0:BANK], scalar1=-1.0, scalar2=shift[t][:], op0=ALU.mult, op1=ALU.add
            )
            nc.scalar.activation(
                out=result[:, BANK:V], in_=neg_z[t][:, BANK:V], func=ACT.Identity, bias=shift[t][:], scale=-1.0
            )
            for h in range(VH):
                half = slice(h * BANK, (h + 1) * BANK)
                nc.sync.dma_start(out[t * P : (t + 1) * P, half], result[:, half])

        for step in range(TB + LAG):
            if step < TB:
                complete(step)
                evacuate(step)
                log_sum_exp(step)
            if step >= LAG:
                finish(step - LAG)
